import numpy as np
import ml_dtypes


def mxq(x, axis, fmt="e4m3"):
    dtype, down = {"e4m3": (ml_dtypes.float8_e4m3fn, 7), "e5m2": (ml_dtypes.float8_e5m2, 14)}[fmt]
    v = np.moveaxis(np.asarray(x, np.float32).astype(ml_dtypes.bfloat16).astype(np.float64), axis, -1)
    blocks = v.reshape(v.shape[:-1] + (-1, 32))
    amax = np.abs(blocks).max(-1, keepdims=True)
    byte = np.maximum(np.where(amax > 0, np.frexp(amax)[1] - 1 + 127, 0) - down, 1)
    scale = np.exp2(byte - 127.0)
    codes = (blocks / scale).astype(np.float32).astype(dtype).astype(np.float64)
    return np.moveaxis((codes * scale).reshape(v.shape), -1, axis)


WIDE = False


def mx_kscale(k):
    if not WIDE:
        return np.ones(k)
    levels = np.array([10, -10, 5, -5, 0])
    a = np.random.permutation(np.resize(levels, k // 512 * 4)).reshape(k // 512, 4)
    idx = np.arange(k)
    return np.exp2(a[idx // 512, idx % 128 // 32])


BF16 = ml_dtypes.bfloat16


def bf(x):
    return np.asarray(x, np.float32).astype(BF16)


def f64(x):
    return np.asarray(x).astype(np.float64)


N, L, H, E, HEADS, R = 512, 16, 512, 1024, 1, 4
EPS = 1e-12


def l2norm(v):
    n = np.sqrt((v * v).sum(-1, keepdims=True))
    return v / np.maximum(n, EPS)


def setup_inputs():
    s = mx_kscale(H)
    gloss = np.random.standard_normal((N, 1, H))
    amp_w = 0.5 + np.random.random_sample((N, L, 1))
    amp_s = 0.5 + np.random.random_sample((N, 1))
    feature = amp_w * 0.7 * (gloss + np.random.standard_normal((N, L, H)))
    aspect_v = amp_s * np.random.standard_normal((N, H))
    return {"feature": bf(feature * s), "aspect_v": bf(aspect_v * s),
            "W": bf(np.random.standard_normal((HEADS, E, H)) / np.sqrt(H) / s),
            "b": bf(0.2 * np.random.standard_normal((HEADS, E)))}


def reference(feature, aspect_v, W, b):
    wt = mxq(f64(W).transpose(0, 2, 1), 1, "e4m3")
    bias = f64(b)
    q = (mxq(f64(aspect_v), 1, "e4m3") @ wt) + bias[:, None, :]
    fh = (mxq(f64(feature), 2, "e4m3").reshape(N * L, H) @ wt).reshape(HEADS, N, L, E) + bias[:, None, None, :]
    return l2norm(q), l2norm(fh).mean(axis=2)

@@ -1,0 +1,238 @@
+from contextlib import ExitStack
+
+import concourse.mybir as mybir
+from concourse.masks import make_identity
+
+F32 = mybir.dt.float32
+BF16 = mybir.dt.bfloat16
+U32 = mybir.dt.uint32
+U8 = mybir.dt.uint8
+FP8X4 = mybir.dt.float8_e4m3fn_x4
+ALU = mybir.AluOpType
+ACT = mybir.ActivationFunctionType
+
+P = 128
+SENSES, WORDS, H, E = 512, 16, 512, 1024
+EPS = 1e-12
+N_TILE = 512
+HALVES = E // N_TILE
+BATCH = 4
+GROUPS = SENSES // P
+BATCHES_PER_GROUP = WORDS // BATCH
+N_BATCHES = 1 + GROUPS * BATCHES_PER_GROUP
+HALF_WORDS = H // 4
+
+ON_TENSOR, ON_GPSIMD, ON_VECTOR = 0, 1, 2
+
+
+def pooling_engine(word):
+    return ((word + 1) % 8) % 3
+
+
+def words_on(engine):
+    return [word for word in range(WORDS) if pooling_engine(word) == engine]
+
+
+FLOPS = 2 * (SENSES * WORDS + SENSES) * H * E
+
+
+def tile_biencodermodel_pa_t_kernel(tc, feature, aspect_v, W, b, out_0, out_1):
+    nc = tc.nc
+    with ExitStack() as stack:
+        const = stack.enter_context(tc.tile_pool(name="const", bufs=1))
+        rows_pool = stack.enter_context(tc.tile_pool(name="rows", bufs=1))
+        mx_pool = stack.enter_context(tc.tile_pool(name="mx", bufs=3))
+        y_pool = stack.enter_context(tc.tile_pool(name="ypool", bufs=14))
+        scratch_pool = stack.enter_context(tc.tile_pool(name="scratch", bufs=4))
+        stats_pool = stack.enter_context(tc.tile_pool(name="stats", bufs=6))
+        result_pool = stack.enter_context(tc.tile_pool(name="result", bufs=2))
+        t_psum = stack.enter_context(tc.psum_pool(name="tpsum", bufs=2))
+        a_psum = stack.enter_context(tc.psum_pool(name="apsum", bufs=4))
+        p_psum = stack.enter_context(tc.psum_pool(name="ppsum", bufs=1))
+        stack.enter_context(tc.manual_schedule())
+
+        def load_batch(name, src):
+            raw = rows_pool.tile([P, BATCH * H], BF16, name=name)
+            nc.sync.dma_start(out=raw[:].rearrange("p (t k) -> p t k", t=BATCH), in_=src)
+            return raw
+
+        bias = const.tile([P, E], BF16)
+        nc.scalar.dma_start(out=bias[:], in_=b.rearrange("o e -> (o e)").partition_broadcast(P))
+        ident = const.tile([P, P], F32)
+        make_identity(nc, ident[:])
+
+        w_raw = [
+            load_batch(
+                "w_raw%d" % j,
+                W[0, j * BATCH * P : (j + 1) * BATCH * P, :].rearrange("(t p) k -> p t k", p=P),
+            )
+            for j in range(HALVES)
+        ]
+        raws = [load_batch("q_raw", aspect_v.rearrange("(t p) k -> p t k", p=P))]
+        for group in range(GROUPS):
+            for part in range(BATCHES_PER_GROUP):
+                raws.append(
+                    load_batch(
+                        "f_raw%d_%d" % (group, part),
+                        feature[group * P : (group + 1) * P, part * BATCH : (part + 1) * BATCH, :],
+                    )
+                )
+
+        def transpose_and_regroup(raw):
+            words = raw[:].bitcast(F32)
+            grouped = mx_pool.tile([P, BATCH * P * 4], BF16, align_bytes=64)
+            grouped_words = grouped[:].bitcast(F32).rearrange(
+                "p (t r u) -> p t r u", t=BATCH, r=P, u=2
+            )
+            for pair in range(BATCH // 2):
+                flipped = t_psum.tile([P, 2, 2, P], F32)
+                for t in range(2):
+                    for u in range(2):
+                        first = ((2 * pair + t) * 2 + u) * HALF_WORDS
+                        nc.tensor.transpose(
+                            flipped[:, t, u, :], words[:, first : first + HALF_WORDS], ident[:]
+                        )
+                nc.scalar.copy(
+                    out=grouped_words[:, 2 * pair : 2 * pair + 2, :, :],
+                    in_=flipped[:].rearrange("p t u r -> p t r u"),
+                )
+            return grouped
+
+        def quantise(grouped, codes, scales):
+            nc.vector.quantize_mx(out=codes.bitcast(FP8X4), scales=scales, in_=grouped[:])
+
+        def quantise_batch(grouped):
+            codes = mx_pool.tile([P, BATCH * P], U32, align_bytes=64)
+            scales = mx_pool.tile([P, BATCH * P], U8, align_bytes=64)
+            quantise(grouped, codes[:], scales[:])
+            return codes, scales
+
+        w_codes = const.tile([P, E], U32, align_bytes=64)
+        w_scales = const.tile([P, E], U8, align_bytes=64)
+
+        def project(operand, t, sumsq):
+            codes, scales = operand
+            rows = slice(t * P, (t + 1) * P)
+            y = y_pool.tile([P, E], F32)
+            for h in range(HALVES):
+                cols = slice(h * N_TILE, (h + 1) * N_TILE)
+                acc = a_psum.tile([P, N_TILE], F32)
+                nc.tensor.matmul_mx(
+                    out=acc[:],
+                    lhsT=codes[:, rows].bitcast(FP8X4),
+                    lhsT_scale=scales[:, rows],
+                    rhs=w_codes[:, cols].bitcast(FP8X4),
+                    rhs_scale=w_scales[:, cols],
+                    start=True,
+                    stop=True,
+                )
+                nc.vector.tensor_tensor(out=y[:, cols], in0=acc[:], in1=bias[:, cols], op=ALU.add)
+            squares = scratch_pool.tile([P, E], BF16)
+            nc.scalar.activation(
+                out=squares[:], in_=y[:], func=ACT.Square, accum_out=sumsq[:, t : t + 1]
+            )
+            return y
+
+        def norms(sumsq, count):
+            floored = stats_pool.tile([P, BATCH], F32)
+            nc.vector.tensor_scalar_max(out=floored[:], in0=sumsq[:], scalar1=EPS * EPS)
+            norm = stats_pool.tile([P, BATCH], F32)
+            nc.scalar.activation(out=norm[:], in_=floored[:], func=ACT.Sqrt, scale=float(count * count))
+            return norm
+
+        def weights(batch, norm):
+            inv = stats_pool.tile([P, BATCH], F32)
+            nc.vector.reciprocal(out=inv[:], in_=norm[:])
+            diags = {}
+            for t in range(BATCH):
+                if batch > 0 and pooling_engine(((batch - 1) % BATCHES_PER_GROUP) * BATCH + t) == ON_TENSOR:
+                    diag = stats_pool.tile([P, P], F32)
+                    nc.gpsimd.tensor_scalar(
+                        out=diag[:], in0=ident[:], scalar1=inv[:, t : t + 1], scalar2=0.0,
+                        op0=ALU.mult, op1=ALU.add,
+                    )
+                    diags[t] = diag
+            return inv, diags
+
+        def store_unit(t, y, weight):
+            unit = result_pool.tile([P, E], F32)
+            nc.gpsimd.tensor_scalar(
+                out=unit[:], in0=y[:], scalar1=weight, scalar2=0.0, op0=ALU.mult, op1=ALU.add
+            )
+            nc.sync.dma_start(out=out_0[0, t * P : (t + 1) * P, :], in_=unit[:])
+
+        sums = {}
+
+        def pool_word(group, word, y, weight, diag):
+            engine = pooling_engine(word)
+            first = word == words_on(engine)[0]
+            last = word == words_on(engine)[-1]
+            if word == 0:
+                sums[ON_TENSOR] = p_psum.tile([P, HALVES, N_TILE], F32, name="sum_t")
+                sums[ON_GPSIMD] = result_pool.tile([P, E], F32, name="sum_g")
+                sums[ON_VECTOR] = result_pool.tile([P, E], F32, name="sum_v")
+            if engine == ON_TENSOR:
+                for h in range(HALVES):
+                    nc.tensor.matmul(
+                        out=sums[ON_TENSOR][:, h, :],
+                        lhsT=diag[:],
+                        rhs=y[:, h * N_TILE : (h + 1) * N_TILE],
+                        start=first,
+                        stop=last,
+                    )
+            elif engine == ON_GPSIMD:
+                scaled = sums[ON_GPSIMD] if first else y
+                nc.gpsimd.tensor_scalar(
+                    out=scaled[:], in0=y[:], scalar1=weight, scalar2=0.0, op0=ALU.mult, op1=ALU.add
+                )
+                if not first:
+                    nc.gpsimd.tensor_tensor(
+                        out=sums[ON_GPSIMD][:], in0=sums[ON_GPSIMD][:], in1=y[:], op=ALU.add
+                    )
+            elif first:
+                nc.vector.tensor_scalar_mul(out=sums[ON_VECTOR][:], in0=y[:], scalar1=weight)
+            else:
+                nc.vector.scalar_tensor_tensor(
+                    out=sums[ON_VECTOR][:], in0=y[:], scalar=weight, in1=sums[ON_VECTOR][:],
+                    op0=ALU.mult, op1=ALU.add,
+                )
+            if word == WORDS - 1:
+                mean = result_pool.tile([P, E], F32)
+                for h in range(HALVES):
+                    cols = slice(h * N_TILE, (h + 1) * N_TILE)
+                    nc.vector.tensor_tensor(
+                        out=mean[:, cols], in0=sums[ON_TENSOR][:, h, :], in1=sums[ON_VECTOR][:, cols],
+                        op=ALU.add,
+                    )
+                nc.gpsimd.tensor_tensor(out=mean[:], in0=mean[:], in1=sums[ON_GPSIMD][:], op=ALU.add)
+                nc.sync.dma_start(out=out_1[0, group * P : (group + 1) * P, :], in_=mean[:])
+
+        w_grouped = [transpose_and_regroup(w_raw[j]) for j in range(HALVES)]
+        grouped = {0: transpose_and_regroup(raws[0])}
+        for j in range(HALVES):
+            cols = slice(j * N_TILE, (j + 1) * N_TILE)
+            quantise(w_grouped[j], w_codes[:, cols], w_scales[:, cols])
+        grouped[1] = transpose_and_regroup(raws[1])
+        operands = {0: quantise_batch(grouped[0])}
+        ys, sumsqs, norm_of, weight_of = {}, {}, {}, {}
+
+        for i in range(N_BATCHES + 2):
+            if i + 2 < N_BATCHES:
+                grouped[i + 2] = transpose_and_regroup(raws[i + 2])
+            if i + 1 < N_BATCHES:
+                operands[i + 1] = quantise_batch(grouped[i + 1])
+            if i < N_BATCHES:
+                sumsqs[i] = stats_pool.tile([P, BATCH], F32, name="sumsq")
+            for t in range(BATCH):
+                if i < N_BATCHES:
+                    ys[i, t] = project(operands[i], t, sumsqs[i])
+                if t == 0 and 0 <= i - 1 < N_BATCHES:
+                    norm_of[i - 1] = norms(sumsqs[i - 1], 1 if i - 1 == 0 else WORDS)
+                if t == 2 and 0 <= i - 1 < N_BATCHES:
+                    weight_of[i - 1] = weights(i - 1, norm_of[i - 1])
+                if i - 2 == 0:
+                    store_unit(t, ys[0, t], weight_of[0][0][:, t : t + 1])
+                elif 0 < i - 2 < N_BATCHES:
+                    group, part = divmod(i - 3, BATCHES_PER_GROUP)
+                    inv, diags = weight_of[i - 2]
+                    pool_word(group, part * BATCH + t, ys[i - 2, t], inv[:, t : t + 1], diags.get(t))

@@ -22,11 +22,11 @@ BATCHES_PER_GROUP = WORDS // BATCH
 N_BATCHES = 1 + GROUPS * BATCHES_PER_GROUP
 HALF_WORDS = H // 4
 
-ON_TENSOR, ON_GPSIMD, ON_VECTOR = 0, 1, 2
+ON_VECTOR, ON_TENSOR, ON_GPSIMD = 0, 1, 2
 
 
 def pooling_engine(word):
-    return ((word + 1) % 8) % 3
+    return word % 3
 
 
 def words_on(engine):
@@ -147,10 +147,7 @@ def tile_biencodermodel_pa_t_kernel(tc, feature, aspect_v, W, b, out_0, out_1):
             for t in range(BATCH):
                 if batch > 0 and pooling_engine(((batch - 1) % BATCHES_PER_GROUP) * BATCH + t) == ON_TENSOR:
                     diag = stats_pool.tile([P, P], F32)
-                    nc.gpsimd.tensor_scalar(
-                        out=diag[:], in0=ident[:], scalar1=inv[:, t : t + 1], scalar2=0.0,
-                        op0=ALU.mult, op1=ALU.add,
-                    )
+                    nc.scalar.activation(out=diag[:], in_=ident[:], func=ACT.Copy, scale=inv[:, t : t + 1])
                     diags[t] = diag
             return inv, diags
 
@@ -197,15 +194,16 @@ def tile_biencodermodel_pa_t_kernel(tc, feature, aspect_v, W, b, out_0, out_1):
                     op0=ALU.mult, op1=ALU.add,
                 )
             if word == WORDS - 1:
-                mean = result_pool.tile([P, E], F32)
                 for h in range(HALVES):
                     cols = slice(h * N_TILE, (h + 1) * N_TILE)
                     nc.vector.tensor_tensor(
-                        out=mean[:, cols], in0=sums[ON_TENSOR][:, h, :], in1=sums[ON_VECTOR][:, cols],
-                        op=ALU.add,
+                        out=sums[ON_VECTOR][:, cols], in0=sums[ON_TENSOR][:, h, :],
+                        in1=sums[ON_VECTOR][:, cols], op=ALU.add,
                     )
-                nc.gpsimd.tensor_tensor(out=mean[:], in0=mean[:], in1=sums[ON_GPSIMD][:], op=ALU.add)
-                nc.sync.dma_start(out=out_1[0, group * P : (group + 1) * P, :], in_=mean[:])
+
+        def store_mean(group, sum_v, sum_g):
+            nc.vector.tensor_tensor(out=sum_v[:], in0=sum_v[:], in1=sum_g[:], op=ALU.add)
+            nc.sync.dma_start(out=out_1[0, group * P : (group + 1) * P, :], in_=sum_v[:])
 
         w_grouped = [transpose_and_regroup(w_raw[j]) for j in range(HALVES)]
         grouped = {0: transpose_and_regroup(raws[0])}
@@ -236,3 +234,8 @@ def tile_biencodermodel_pa_t_kernel(tc, feature, aspect_v, W, b, out_0, out_1):
                     group, part = divmod(i - 3, BATCHES_PER_GROUP)
                     inv, diags = weight_of[i - 2]
                     pool_word(group, part * BATCH + t, ys[i - 2, t], inv[:, t : t + 1], diags.get(t))
+                    if part == BATCHES_PER_GROUP - 1 and t == BATCH - 1:
+                        finished = (group, sums[ON_VECTOR], sums[ON_GPSIMD])
+                    if part == 0 and t == 1 and group > 0:
+                        store_mean(*finished)
+        store_mean(*finished)

@@ -18,15 +18,18 @@ N_TILE = 512
 HALVES = E // N_TILE
 BATCH = 4
 GROUPS = SENSES // P
-BATCHES_PER_GROUP = WORDS // BATCH
-N_BATCHES = 1 + GROUPS * BATCHES_PER_GROUP
+F_TILES = GROUPS * WORDS
+N_TILES = F_TILES + GROUPS
+N_BATCHES = N_TILES // BATCH
 HALF_WORDS = H // 4
+LAG = 2 * BATCH
 
 ON_VECTOR, ON_TENSOR, ON_GPSIMD = 0, 1, 2
+GPSIMD_WORDS = 5
 
 
 def pooling_engine(word):
-    return word % 3
+    return ON_GPSIMD if word < GPSIMD_WORDS else word % 2
 
 
 def words_on(engine):
@@ -42,7 +45,7 @@ def tile_biencodermodel_pa_t_kernel(tc, feature, aspect_v, W, b, out_0, out_1):
         const = stack.enter_context(tc.tile_pool(name="const", bufs=1))
         rows_pool = stack.enter_context(tc.tile_pool(name="rows", bufs=1))
         mx_pool = stack.enter_context(tc.tile_pool(name="mx", bufs=3))
-        y_pool = stack.enter_context(tc.tile_pool(name="ypool", bufs=14))
+        y_pool = stack.enter_context(tc.tile_pool(name="ypool", bufs=18))
         scratch_pool = stack.enter_context(tc.tile_pool(name="scratch", bufs=4))
         stats_pool = stack.enter_context(tc.tile_pool(name="stats", bufs=6))
         result_pool = stack.enter_context(tc.tile_pool(name="result", bufs=2))
@@ -68,15 +71,16 @@ def tile_biencodermodel_pa_t_kernel(tc, feature, aspect_v, W, b, out_0, out_1):
             )
             for j in range(HALVES)
         ]
-        raws = [load_batch("q_raw", aspect_v.rearrange("(t p) k -> p t k", p=P))]
+        raws = []
         for group in range(GROUPS):
-            for part in range(BATCHES_PER_GROUP):
+            for first_word in range(0, WORDS, BATCH):
                 raws.append(
                     load_batch(
-                        "f_raw%d_%d" % (group, part),
-                        feature[group * P : (group + 1) * P, part * BATCH : (part + 1) * BATCH, :],
+                        "f_raw%d_%d" % (group, first_word),
+                        feature[group * P : (group + 1) * P, first_word : first_word + BATCH, :],
                     )
                 )
+        raws.append(load_batch("q_raw", aspect_v.rearrange("(t p) k -> p t k", p=P)))
 
         def transpose_and_regroup(raw):
             words = raw[:].bitcast(F32)
@@ -110,10 +114,10 @@ def tile_biencodermodel_pa_t_kernel(tc, feature, aspect_v, W, b, out_0, out_1):
         w_codes = const.tile([P, E], U32, align_bytes=64)
         w_scales = const.tile([P, E], U8, align_bytes=64)
 
-        def project(operand, t, sumsq):
+        def multiply(operand, t):
             codes, scales = operand
             rows = slice(t * P, (t + 1) * P)
-            y = y_pool.tile([P, E], F32)
+            products = []
             for h in range(HALVES):
                 cols = slice(h * N_TILE, (h + 1) * N_TILE)
                 acc = a_psum.tile([P, N_TILE], F32)
@@ -126,11 +130,16 @@ def tile_biencodermodel_pa_t_kernel(tc, feature, aspect_v, W, b, out_0, out_1):
                     start=True,
                     stop=True,
                 )
-                nc.vector.tensor_tensor(out=y[:, cols], in0=acc[:], in1=bias[:, cols], op=ALU.add)
+                products.append(acc)
+            return products
+
+        def add_bias_and_square(products, sumsq_column):
+            y = y_pool.tile([P, E], F32)
+            for h in range(HALVES):
+                cols = slice(h * N_TILE, (h + 1) * N_TILE)
+                nc.vector.tensor_tensor(out=y[:, cols], in0=products[h][:], in1=bias[:, cols], op=ALU.add)
             squares = scratch_pool.tile([P, E], BF16)
-            nc.scalar.activation(
-                out=squares[:], in_=y[:], func=ACT.Square, accum_out=sumsq[:, t : t + 1]
-            )
+            nc.scalar.activation(out=squares[:], in_=y[:], func=ACT.Square, accum_out=sumsq_column)
             return y
 
         def norms(sumsq, count):
@@ -145,7 +154,8 @@ def tile_biencodermodel_pa_t_kernel(tc, feature, aspect_v, W, b, out_0, out_1):
             nc.vector.reciprocal(out=inv[:], in_=norm[:])
             diags = {}
             for t in range(BATCH):
-                if batch > 0 and pooling_engine(((batch - 1) % BATCHES_PER_GROUP) * BATCH + t) == ON_TENSOR:
+                s = batch * BATCH + t
+                if s < F_TILES and pooling_engine(s % WORDS) == ON_TENSOR:
                     diag = stats_pool.tile([P, P], F32)
                     nc.scalar.activation(out=diag[:], in_=ident[:], func=ACT.Copy, scale=inv[:, t : t + 1])
                     diags[t] = diag
@@ -153,14 +163,12 @@ def tile_biencodermodel_pa_t_kernel(tc, feature, aspect_v, W, b, out_0, out_1):
 
         def store_unit(t, y, weight):
             unit = result_pool.tile([P, E], F32)
-            nc.gpsimd.tensor_scalar(
-                out=unit[:], in0=y[:], scalar1=weight, scalar2=0.0, op0=ALU.mult, op1=ALU.add
-            )
+            nc.vector.tensor_scalar_mul(out=unit[:], in0=y[:], scalar1=weight)
             nc.sync.dma_start(out=out_0[0, t * P : (t + 1) * P, :], in_=unit[:])
 
         sums = {}
 
-        def pool_word(group, word, y, weight, diag):
+        def pool_word(word, y, weight, diag):
             engine = pooling_engine(word)
             first = word == words_on(engine)[0]
             last = word == words_on(engine)[-1]
@@ -193,17 +201,16 @@ def tile_biencodermodel_pa_t_kernel(tc, feature, aspect_v, W, b, out_0, out_1):
                     out=sums[ON_VECTOR][:], in0=y[:], scalar=weight, in1=sums[ON_VECTOR][:],
                     op0=ALU.mult, op1=ALU.add,
                 )
-            if word == WORDS - 1:
-                for h in range(HALVES):
-                    cols = slice(h * N_TILE, (h + 1) * N_TILE)
-                    nc.vector.tensor_tensor(
-                        out=sums[ON_VECTOR][:, cols], in0=sums[ON_TENSOR][:, h, :],
-                        in1=sums[ON_VECTOR][:, cols], op=ALU.add,
-                    )
+            if engine == ON_VECTOR and last:
+                nc.gpsimd.tensor_tensor(
+                    out=sums[ON_GPSIMD][:], in0=sums[ON_GPSIMD][:], in1=sums[ON_VECTOR][:], op=ALU.add
+                )
 
-        def store_mean(group, sum_v, sum_g):
-            nc.vector.tensor_tensor(out=sum_v[:], in0=sum_v[:], in1=sum_g[:], op=ALU.add)
-            nc.sync.dma_start(out=out_1[0, group * P : (group + 1) * P, :], in_=sum_v[:])
+        def store_mean(group, sum_t, sum_g):
+            for h in range(HALVES):
+                cols = slice(h * N_TILE, (h + 1) * N_TILE)
+                nc.vector.tensor_tensor(out=sum_g[:, cols], in0=sum_t[:, h, :], in1=sum_g[:, cols], op=ALU.add)
+            nc.sync.dma_start(out=out_1[0, group * P : (group + 1) * P, :], in_=sum_g[:])
 
         w_grouped = [transpose_and_regroup(w_raw[j]) for j in range(HALVES)]
         grouped = {0: transpose_and_regroup(raws[0])}
@@ -212,30 +219,34 @@ def tile_biencodermodel_pa_t_kernel(tc, feature, aspect_v, W, b, out_0, out_1):
             quantise(w_grouped[j], w_codes[:, cols], w_scales[:, cols])
         grouped[1] = transpose_and_regroup(raws[1])
         operands = {0: quantise_batch(grouped[0])}
+        products = {0: multiply(operands[0], 0)}
         ys, sumsqs, norm_of, weight_of = {}, {}, {}, {}
 
-        for i in range(N_BATCHES + 2):
-            if i + 2 < N_BATCHES:
+        for s in range(N_TILES + LAG + 2):
+            i, t = divmod(s, BATCH)
+            if t == 0 and i + 2 < N_BATCHES:
                 grouped[i + 2] = transpose_and_regroup(raws[i + 2])
-            if i + 1 < N_BATCHES:
+            if t == 0 and i + 1 < N_BATCHES:
                 operands[i + 1] = quantise_batch(grouped[i + 1])
-            if i < N_BATCHES:
-                sumsqs[i] = stats_pool.tile([P, BATCH], F32, name="sumsq")
-            for t in range(BATCH):
-                if i < N_BATCHES:
-                    ys[i, t] = project(operands[i], t, sumsqs[i])
-                if t == 0 and 0 <= i - 1 < N_BATCHES:
-                    norm_of[i - 1] = norms(sumsqs[i - 1], 1 if i - 1 == 0 else WORDS)
-                if t == 2 and 0 <= i - 1 < N_BATCHES:
-                    weight_of[i - 1] = weights(i - 1, norm_of[i - 1])
-                if i - 2 == 0:
-                    store_unit(t, ys[0, t], weight_of[0][0][:, t : t + 1])
-                elif 0 < i - 2 < N_BATCHES:
-                    group, part = divmod(i - 3, BATCHES_PER_GROUP)
-                    inv, diags = weight_of[i - 2]
-                    pool_word(group, part * BATCH + t, ys[i - 2, t], inv[:, t : t + 1], diags.get(t))
-                    if part == BATCHES_PER_GROUP - 1 and t == BATCH - 1:
-                        finished = (group, sums[ON_VECTOR], sums[ON_GPSIMD])
-                    if part == 0 and t == 1 and group > 0:
-                        store_mean(*finished)
-        store_mean(*finished)
+            if s + 1 < N_TILES:
+                products[s + 1] = multiply(operands[(s + 1) // BATCH], (s + 1) % BATCH)
+            if s < N_TILES:
+                if t == 0:
+                    sumsqs[i] = stats_pool.tile([P, BATCH], F32, name="sumsq")
+                ys[s] = add_bias_and_square(products[s], sumsqs[i][:, t : t + 1])
+            if t == 0 and 0 <= i - 1 < N_BATCHES:
+                norm_of[i - 1] = norms(sumsqs[i - 1], WORDS if (i - 1) * BATCH < F_TILES else 1)
+            if t == 1 and 0 <= i - 1 < N_BATCHES:
+                weight_of[i - 1] = weights(i - 1, norm_of[i - 1])
+            done = s - LAG
+            if 0 <= done < N_TILES:
+                inv, diags = weight_of[done // BATCH]
+                weight = inv[:, done % BATCH : done % BATCH + 1]
+                if done < F_TILES:
+                    pool_word(done % WORDS, ys[done], weight, diags.get(done % BATCH))
+                else:
+                    store_unit(done - F_TILES, ys[done], weight)
+            if 0 <= done - 2 < F_TILES and (done - 2) % WORDS == WORDS - 1:
+                store_mean((done - 2) // WORDS, finished[ON_TENSOR], finished[ON_GPSIMD])
+            if 0 <= done < F_TILES and done % WORDS == WORDS - 1:
+                finished = dict(sums)

@@ -25,11 +25,10 @@ HALF_WORDS = H // 4
 LAG = 2 * BATCH
 
 ON_VECTOR, ON_TENSOR, ON_GPSIMD = 0, 1, 2
-GPSIMD_WORDS = 5
 
 
 def pooling_engine(word):
-    return ON_GPSIMD if word < GPSIMD_WORDS else word % 2
+    return word % 3
 
 
 def words_on(engine):
@@ -45,7 +44,7 @@ def tile_biencodermodel_pa_t_kernel(tc, feature, aspect_v, W, b, out_0, out_1):
         const = stack.enter_context(tc.tile_pool(name="const", bufs=1))
         rows_pool = stack.enter_context(tc.tile_pool(name="rows", bufs=1))
         mx_pool = stack.enter_context(tc.tile_pool(name="mx", bufs=3))
-        y_pool = stack.enter_context(tc.tile_pool(name="ypool", bufs=18))
+        y_pool = stack.enter_context(tc.tile_pool(name="ypool", bufs=14))
         scratch_pool = stack.enter_context(tc.tile_pool(name="scratch", bufs=4))
         stats_pool = stack.enter_context(tc.tile_pool(name="stats", bufs=6))
         result_pool = stack.enter_context(tc.tile_pool(name="result", bufs=2))
@@ -201,16 +200,18 @@ def tile_biencodermodel_pa_t_kernel(tc, feature, aspect_v, W, b, out_0, out_1):
                     out=sums[ON_VECTOR][:], in0=y[:], scalar=weight, in1=sums[ON_VECTOR][:],
                     op0=ALU.mult, op1=ALU.add,
                 )
-            if engine == ON_VECTOR and last:
-                nc.gpsimd.tensor_tensor(
-                    out=sums[ON_GPSIMD][:], in0=sums[ON_GPSIMD][:], in1=sums[ON_VECTOR][:], op=ALU.add
-                )
 
-        def store_mean(group, sum_t, sum_g):
+        def store_mean(group):
             for h in range(HALVES):
                 cols = slice(h * N_TILE, (h + 1) * N_TILE)
-                nc.vector.tensor_tensor(out=sum_g[:, cols], in0=sum_t[:, h, :], in1=sum_g[:, cols], op=ALU.add)
-            nc.sync.dma_start(out=out_1[0, group * P : (group + 1) * P, :], in_=sum_g[:])
+                nc.vector.tensor_tensor(
+                    out=sums[ON_VECTOR][:, cols], in0=sums[ON_TENSOR][:, h, :],
+                    in1=sums[ON_VECTOR][:, cols], op=ALU.add,
+                )
+            nc.gpsimd.tensor_tensor(
+                out=sums[ON_GPSIMD][:], in0=sums[ON_GPSIMD][:], in1=sums[ON_VECTOR][:], op=ALU.add
+            )
+            nc.sync.dma_start(out=out_1[0, group * P : (group + 1) * P, :], in_=sums[ON_GPSIMD][:])
 
         w_grouped = [transpose_and_regroup(w_raw[j]) for j in range(HALVES)]
         grouped = {0: transpose_and_regroup(raws[0])}
@@ -222,7 +223,7 @@ def tile_biencodermodel_pa_t_kernel(tc, feature, aspect_v, W, b, out_0, out_1):
         products = {0: multiply(operands[0], 0)}
         ys, sumsqs, norm_of, weight_of = {}, {}, {}, {}
 
-        for s in range(N_TILES + LAG + 2):
+        for s in range(N_TILES + LAG):
             i, t = divmod(s, BATCH)
             if t == 0 and i + 2 < N_BATCHES:
                 grouped[i + 2] = transpose_and_regroup(raws[i + 2])
@@ -244,9 +245,7 @@ def tile_biencodermodel_pa_t_kernel(tc, feature, aspect_v, W, b, out_0, out_1):
                 weight = inv[:, done % BATCH : done % BATCH + 1]
                 if done < F_TILES:
                     pool_word(done % WORDS, ys[done], weight, diags.get(done % BATCH))
+                    if done % WORDS == WORDS - 1:
+                        store_mean(done // WORDS)
                 else:
                     store_unit(done - F_TILES, ys[done], weight)
-            if 0 <= done - 2 < F_TILES and (done - 2) % WORDS == WORDS - 1:
-                store_mean((done - 2) // WORDS, finished[ON_TENSOR], finished[ON_GPSIMD])
-            if 0 <= done < F_TILES and done % WORDS == WORDS - 1:
-                finished = dict(sums)

from contextlib import ExitStack

import concourse.mybir as mybir
from concourse.masks import make_identity

F32 = mybir.dt.float32
BF16 = mybir.dt.bfloat16
U32 = mybir.dt.uint32
U8 = mybir.dt.uint8
FP8X4 = mybir.dt.float8_e4m3fn_x4
ALU = mybir.AluOpType
ACT = mybir.ActivationFunctionType

P = 128
SENSES, WORDS, H, E = 512, 16, 512, 1024
EPS = 1e-12
N_TILE = 512
HALVES = E // N_TILE
BATCH = 4
GROUPS = SENSES // P
F_TILES = GROUPS * WORDS
N_TILES = F_TILES + GROUPS
N_BATCHES = N_TILES // BATCH
HALF_WORDS = H // 4
LAG = 2 * BATCH

ON_VECTOR, ON_TENSOR, ON_GPSIMD = 0, 1, 2


def pooling_engine(word):
    return word % 3


def words_on(engine):
    return [word for word in range(WORDS) if pooling_engine(word) == engine]


FLOPS = 2 * (SENSES * WORDS + SENSES) * H * E


def tile_biencodermodel_pa_t_kernel(tc, feature, aspect_v, W, b, out_0, out_1):
    nc = tc.nc
    with ExitStack() as stack:
        const = stack.enter_context(tc.tile_pool(name="const", bufs=1))
        rows_pool = stack.enter_context(tc.tile_pool(name="rows", bufs=1))
        mx_pool = stack.enter_context(tc.tile_pool(name="mx", bufs=3))
        y_pool = stack.enter_context(tc.tile_pool(name="ypool", bufs=14))
        scratch_pool = stack.enter_context(tc.tile_pool(name="scratch", bufs=4))
        stats_pool = stack.enter_context(tc.tile_pool(name="stats", bufs=6))
        result_pool = stack.enter_context(tc.tile_pool(name="result", bufs=2))
        t_psum = stack.enter_context(tc.psum_pool(name="tpsum", bufs=2))
        a_psum = stack.enter_context(tc.psum_pool(name="apsum", bufs=4))
        p_psum = stack.enter_context(tc.psum_pool(name="ppsum", bufs=1))
        stack.enter_context(tc.manual_schedule())

        def load_batch(name, src):
            raw = rows_pool.tile([P, BATCH * H], BF16, name=name)
            nc.sync.dma_start(out=raw[:].rearrange("p (t k) -> p t k", t=BATCH), in_=src)
            return raw

        bias = const.tile([P, E], BF16)
        nc.scalar.dma_start(out=bias[:], in_=b.rearrange("o e -> (o e)").partition_broadcast(P))
        ident = const.tile([P, P], F32)
        make_identity(nc, ident[:])

        w_raw = [
            load_batch(
                "w_raw%d" % j,
                W[0, j * BATCH * P : (j + 1) * BATCH * P, :].rearrange("(t p) k -> p t k", p=P),
            )
            for j in range(HALVES)
        ]
        raws = []
        for group in range(GROUPS):
            for first_word in range(0, WORDS, BATCH):
                raws.append(
                    load_batch(
                        "f_raw%d_%d" % (group, first_word),
                        feature[group * P : (group + 1) * P, first_word : first_word + BATCH, :],
                    )
                )
        raws.append(load_batch("q_raw", aspect_v.rearrange("(t p) k -> p t k", p=P)))

        def transpose_and_regroup(raw):
            words = raw[:].bitcast(F32)
            grouped = mx_pool.tile([P, BATCH * P * 4], BF16, align_bytes=64)
            grouped_words = grouped[:].bitcast(F32).rearrange(
                "p (t r u) -> p t r u", t=BATCH, r=P, u=2
            )
            for pair in range(BATCH // 2):
                flipped = t_psum.tile([P, 2, 2, P], F32)
                for t in range(2):
                    for u in range(2):
                        first = ((2 * pair + t) * 2 + u) * HALF_WORDS
                        nc.tensor.transpose(
                            flipped[:, t, u, :], words[:, first : first + HALF_WORDS], ident[:]
                        )
                nc.scalar.copy(
                    out=grouped_words[:, 2 * pair : 2 * pair + 2, :, :],
                    in_=flipped[:].rearrange("p t u r -> p t r u"),
                )
            return grouped

        def quantise(grouped, codes, scales):
            nc.vector.quantize_mx(out=codes.bitcast(FP8X4), scales=scales, in_=grouped[:])

        def quantise_batch(grouped):
            codes = mx_pool.tile([P, BATCH * P], U32, align_bytes=64)
            scales = mx_pool.tile([P, BATCH * P], U8, align_bytes=64)
            quantise(grouped, codes[:], scales[:])
            return codes, scales

        w_codes = const.tile([P, E], U32, align_bytes=64)
        w_scales = const.tile([P, E], U8, align_bytes=64)

        def multiply(operand, t):
            codes, scales = operand
            rows = slice(t * P, (t + 1) * P)
            products = []
            for h in range(HALVES):
                cols = slice(h * N_TILE, (h + 1) * N_TILE)
                acc = a_psum.tile([P, N_TILE], F32)
                nc.tensor.matmul_mx(
                    out=acc[:],
                    lhsT=codes[:, rows].bitcast(FP8X4),
                    lhsT_scale=scales[:, rows],
                    rhs=w_codes[:, cols].bitcast(FP8X4),
                    rhs_scale=w_scales[:, cols],
                    start=True,
                    stop=True,
                )
                products.append(acc)
            return products

        def add_bias_and_square(products, sumsq_column):
            y = y_pool.tile([P, E], F32)
            for h in range(HALVES):
                cols = slice(h * N_TILE, (h + 1) * N_TILE)
                nc.vector.tensor_tensor(out=y[:, cols], in0=products[h][:], in1=bias[:, cols], op=ALU.add)
            squares = scratch_pool.tile([P, E], BF16)
            nc.scalar.activation(out=squares[:], in_=y[:], func=ACT.Square, accum_out=sumsq_column)
            return y

        def norms(sumsq, count):
            floored = stats_pool.tile([P, BATCH], F32)
            nc.vector.tensor_scalar_max(out=floored[:], in0=sumsq[:], scalar1=EPS * EPS)
            norm = stats_pool.tile([P, BATCH], F32)
            nc.scalar.activation(out=norm[:], in_=floored[:], func=ACT.Sqrt, scale=float(count * count))
            return norm

        def weights(batch, norm):
            inv = stats_pool.tile([P, BATCH], F32)
            nc.vector.reciprocal(out=inv[:], in_=norm[:])
            diags = {}
            for t in range(BATCH):
                s = batch * BATCH + t
                if s < F_TILES and pooling_engine(s % WORDS) == ON_TENSOR:
                    diag = stats_pool.tile([P, P], F32)
                    nc.scalar.activation(out=diag[:], in_=ident[:], func=ACT.Copy, scale=inv[:, t : t + 1])
                    diags[t] = diag
            return inv, diags

        def store_unit(t, y, weight):
            unit = result_pool.tile([P, E], F32)
            nc.vector.tensor_scalar_mul(out=unit[:], in0=y[:], scalar1=weight)
            nc.sync.dma_start(out=out_0[0, t * P : (t + 1) * P, :], in_=unit[:])

        sums = {}

        def pool_word(word, y, weight, diag):
            engine = pooling_engine(word)
            first = word == words_on(engine)[0]
            last = word == words_on(engine)[-1]
            if word == 0:
                sums[ON_TENSOR] = p_psum.tile([P, HALVES, N_TILE], F32, name="sum_t")
                sums[ON_GPSIMD] = result_pool.tile([P, E], F32, name="sum_g")
                sums[ON_VECTOR] = result_pool.tile([P, E], F32, name="sum_v")
            if engine == ON_TENSOR:
                for h in range(HALVES):
                    nc.tensor.matmul(
                        out=sums[ON_TENSOR][:, h, :],
                        lhsT=diag[:],
                        rhs=y[:, h * N_TILE : (h + 1) * N_TILE],
                        start=first,
                        stop=last,
                    )
            elif engine == ON_GPSIMD:
                scaled = sums[ON_GPSIMD] if first else y
                nc.gpsimd.tensor_scalar(
                    out=scaled[:], in0=y[:], scalar1=weight, scalar2=0.0, op0=ALU.mult, op1=ALU.add
                )
                if not first:
                    nc.gpsimd.tensor_tensor(
                        out=sums[ON_GPSIMD][:], in0=sums[ON_GPSIMD][:], in1=y[:], op=ALU.add
                    )
            elif first:
                nc.vector.tensor_scalar_mul(out=sums[ON_VECTOR][:], in0=y[:], scalar1=weight)
            else:
                nc.vector.scalar_tensor_tensor(
                    out=sums[ON_VECTOR][:], in0=y[:], scalar=weight, in1=sums[ON_VECTOR][:],
                    op0=ALU.mult, op1=ALU.add,
                )

        def store_mean(group):
            for h in range(HALVES):
                cols = slice(h * N_TILE, (h + 1) * N_TILE)
                nc.vector.tensor_tensor(
                    out=sums[ON_VECTOR][:, cols], in0=sums[ON_TENSOR][:, h, :],
                    in1=sums[ON_VECTOR][:, cols], op=ALU.add,
                )
            nc.gpsimd.tensor_tensor(
                out=sums[ON_GPSIMD][:], in0=sums[ON_GPSIMD][:], in1=sums[ON_VECTOR][:], op=ALU.add
            )
            nc.sync.dma_start(out=out_1[0, group * P : (group + 1) * P, :], in_=sums[ON_GPSIMD][:])

        w_grouped = [transpose_and_regroup(w_raw[j]) for j in range(HALVES)]
        grouped = {0: transpose_and_regroup(raws[0])}
        for j in range(HALVES):
            cols = slice(j * N_TILE, (j + 1) * N_TILE)
            quantise(w_grouped[j], w_codes[:, cols], w_scales[:, cols])
        grouped[1] = transpose_and_regroup(raws[1])
        operands = {0: quantise_batch(grouped[0])}
        products = {0: multiply(operands[0], 0)}
        ys, sumsqs, norm_of, weight_of = {}, {}, {}, {}

        for s in range(N_TILES + LAG):
            i, t = divmod(s, BATCH)
            if t == 0 and i + 2 < N_BATCHES:
                grouped[i + 2] = transpose_and_regroup(raws[i + 2])
            if t == 0 and i + 1 < N_BATCHES:
                operands[i + 1] = quantise_batch(grouped[i + 1])
            if s + 1 < N_TILES:
                products[s + 1] = multiply(operands[(s + 1) // BATCH], (s + 1) % BATCH)
            if s < N_TILES:
                if t == 0:
                    sumsqs[i] = stats_pool.tile([P, BATCH], F32, name="sumsq")
                ys[s] = add_bias_and_square(products[s], sumsqs[i][:, t : t + 1])
            if t == 0 and 0 <= i - 1 < N_BATCHES:
                norm_of[i - 1] = norms(sumsqs[i - 1], WORDS if (i - 1) * BATCH < F_TILES else 1)
            if t == 1 and 0 <= i - 1 < N_BATCHES:
                weight_of[i - 1] = weights(i - 1, norm_of[i - 1])
            done = s - LAG
            if 0 <= done < N_TILES:
                inv, diags = weight_of[done // BATCH]
                weight = inv[:, done % BATCH : done % BATCH + 1]
                if done < F_TILES:
                    pool_word(done % WORDS, ys[done], weight, diags.get(done % BATCH))
                    if done % WORDS == WORDS - 1:
                        store_mean(done // WORDS)
                else:
                    store_unit(done - F_TILES, ys[done], weight)
